import numpy as np
import ml_dtypes


def mxq(x, axis, fmt="e4m3"):
    dtype, down = {"e4m3": (ml_dtypes.float8_e4m3fn, 7), "e5m2": (ml_dtypes.float8_e5m2, 14)}[fmt]
    v = np.moveaxis(np.asarray(x, np.float32).astype(ml_dtypes.bfloat16).astype(np.float64), axis, -1)
    blocks = v.reshape(v.shape[:-1] + (-1, 32))
    amax = np.abs(blocks).max(-1, keepdims=True)
    byte = np.maximum(np.where(amax > 0, np.frexp(amax)[1] - 1 + 127, 0) - down, 1)
    scale = np.exp2(byte - 127.0)
    codes = (blocks / scale).astype(np.float32).astype(dtype).astype(np.float64)
    return np.moveaxis((codes * scale).reshape(v.shape), -1, axis)


WIDE = False


def mx_kscale(k):
    if not WIDE:
        return np.ones(k)
    levels = np.array([10, -10, 5, -5, 0])
    a = np.random.permutation(np.resize(levels, k // 512 * 4)).reshape(k // 512, 4)
    idx = np.arange(k)
    return np.exp2(a[idx // 512, idx % 128 // 32])


BF16 = ml_dtypes.bfloat16


def bf(x):
    return np.asarray(x, np.float32).astype(BF16)


def f64(x):
    return np.asarray(x).astype(np.float64)


B, S, E, P, H = 2, 512, 1024, 1024, 8
D = P // H


def rope(x):
    inv_freq = 1.0 / (10000.0 ** (f64(np.arange(0, D, 2)) / D))
    t = f64(np.arange(S))
    freqs = np.repeat(t[:, None] * inv_freq[None, :], 2, axis=-1)
    cos, sin = np.cos(freqs), np.sin(freqs)
    xp = x.reshape(*x.shape[:-1], D // 2, 2)
    rot = np.stack((-xp[..., 1], xp[..., 0]), axis=-1).reshape(x.shape)
    return x * cos + rot * sin


def setup_inputs():
    s = mx_kscale(E)
    return {"emb": bf(np.random.standard_normal((B, S, E)) * s),
            "W1": bf(np.random.standard_normal((P, E)) * 0.6 / np.sqrt(E) / s),
            "W2": bf(np.random.standard_normal((P, E)) * 0.6 / np.sqrt(E) / s),
            "W3": bf(np.random.standard_normal((P, E)) * 2.0 / np.sqrt(E) / s)}


def reference(emb, W1, W2, W3):
    xq = mxq(f64(emb), 2, "e4m3")
    q = (xq @ mxq(f64(W1), 1, "e4m3").T).reshape(B, H, S, D)
    k = (xq @ mxq(f64(W2), 1, "e4m3").T).reshape(B, H, S, D)
    v = (xq @ mxq(f64(W3), 1, "e4m3").T).reshape(B, H, S, D)
    return rope(q), rope(k), v

@@ -1,0 +1,241 @@
+import math
+from contextlib import ExitStack
+
+import concourse.mybir as mybir
+from concourse.masks import make_identity
+
+FLOPS = 2 * 1024 * 1024 * 3072
+
+MANUAL = False
+
+F32 = mybir.dt.float32
+BF16 = mybir.dt.bfloat16
+I32 = mybir.dt.int32
+U32 = mybir.dt.uint32
+U8 = mybir.dt.uint8
+FP8X4 = mybir.dt.float8_e4m3fn_x4
+ALU = mybir.AluOpType
+ACT = mybir.ActivationFunctionType
+
+P = 128
+
+
+def tile_attention_pa_kernel(tc, emb, W1, W2, W3, out_0, out_1, out_2):
+    nc = tc.nc
+    x2d = emb.flatten_outer_dims()
+    weights = [W1, W2, W3]
+    outs = [o.rearrange("b h (a c) d -> (b h a) (c d)", c=8) for o in (out_0, out_1, out_2)]
+
+    with ExitStack() as ctx:
+        const = ctx.enter_context(tc.tile_pool(name="const", bufs=1))
+        gwp = ctx.enter_context(tc.tile_pool(name="gwp", bufs=2))
+        prodp = ctx.enter_context(tc.tile_pool(name="prodp", bufs=3))
+        yp = ctx.enter_context(tc.tile_pool(name="yp", bufs=9))
+        vp = ctx.enter_context(tc.tile_pool(name="vp", bufs=3))
+        tps = ctx.enter_context(tc.psum_pool(name="tps", bufs=4))
+        accp = ctx.enter_context(tc.psum_pool(name="accp", bufs=3))
+        accvp = ctx.enter_context(tc.psum_pool(name="accvp", bufs=1))
+        if MANUAL:
+            ctx.enter_context(tc.manual_schedule())
+
+        xs = const.tile([P, 8192], BF16, name="xs")
+        ws = [const.tile([P, 4096], BF16, name="ws%d" % g) for g in range(6)]
+        gx = const.tile([P, 8192], BF16, name="gx", align_bytes=64)
+        cx = const.tile([P, 2048], U32, name="cx", align_bytes=64)
+        sx = const.tile([P, 2048], U8, name="sx", align_bytes=64)
+        cw = [const.tile([P, 1024], U32, name="cw%d" % g, align_bytes=64) for g in range(6)]
+        sw = [const.tile([P, 1024], U8, name="sw%d" % g, align_bytes=64) for g in range(6)]
+        ident = const.tile([P, P], F32, name="ident")
+        pos = const.tile([P, 8], F32, name="pos")
+        post = const.tile([P, 8], F32, name="post")
+        freq = const.tile([P, 64], F32, name="freq")
+        warm = const.tile([P, 1], F32, name="warm")
+        turns = const.tile([P, 512], F32, name="turns")
+        whole_i = const.tile([P, 512], I32, name="whole_i")
+        whole_f = const.tile([P, 512], F32, name="whole_f")
+        tab = const.tile([P, 2048], F32, name="tab")
+
+        xs_w = xs.bitcast(F32)
+        gx_w = gx.bitcast(F32)
+
+        def load_x(j0, j1):
+            nc.sync.dma_start(
+                out=xs[:, 1024 * j0 : 1024 * j1].rearrange("p (j k) -> p j k", k=1024),
+                in_=x2d[P * j0 : P * j1, :].rearrange("(j p) k -> p j k", p=P),
+            )
+
+        def load_w(g, j0, j1):
+            r0 = 512 * (g % 2)
+            nc.sync.dma_start(
+                out=ws[g][:, 1024 * j0 : 1024 * j1].rearrange("p (j k) -> p j k", k=1024),
+                in_=weights[g // 2][r0 + P * j0 : r0 + P * j1, :].rearrange("(j p) k -> p j k", p=P),
+            )
+
+        load_x(0, 2)
+        load_w(0, 0, 2)
+        load_w(0, 2, 4)
+        load_x(2, 4)
+        load_x(4, 6)
+        load_x(6, 8)
+        for g in range(1, 6):
+            load_w(g, 0, 4)
+
+        nc.vector.memset(warm, 0.0)
+        nc.scalar.activation(out=warm, in_=warm, func=ACT.Sin)
+        nc.gpsimd.iota(pos[0:64, :], pattern=[[1, 8]], base=0, channel_multiplier=8,
+                       allow_small_or_imprecise_dtypes=True)
+        nc.gpsimd.iota(pos[64:128, :], pattern=[[1, 8]], base=0, channel_multiplier=8,
+                       allow_small_or_imprecise_dtypes=True)
+        make_identity(nc, ident)
+
+        ratio = 10000.0 ** (-1.0 / 64.0)
+        nc.vector.memset(freq[:, 0:1], 1.0)
+        for e in range(6):
+            w = 2 ** e
+            nc.vector.tensor_scalar_mul(out=freq[:, w : 2 * w], in0=freq[:, 0:w], scalar1=ratio ** w)
+        nc.vector.tensor_scalar_mul(out=post, in0=pos, scalar1=1.0 / (2.0 * math.pi))
+        nc.vector.tensor_tensor(
+            out=turns.rearrange("p (c i) -> p c i", c=8),
+            in0=post.unsqueeze(2).to_broadcast([P, 8, 64]),
+            in1=freq.unsqueeze(1).to_broadcast([P, 8, 64]),
+            op=ALU.mult,
+        )
+        nc.vector.tensor_scalar_add(out=whole_i, in0=turns, scalar1=0.125)
+        nc.vector.tensor_copy(out=whole_f, in_=whole_i)
+        phase = prodp.tile([P, 1024], F32, name="phase", tag="prod")
+        nc.vector.tensor_tensor(out=phase[:, 0:512], in0=turns, in1=whole_f, op=ALU.subtract)
+        nc.vector.tensor_scalar_add(out=phase[:, 512:1024], in0=phase[:, 0:512], scalar1=-0.25)
+        half_sin = prodp.tile([P, 1024], F32, name="half_sin", tag="prod")
+        nc.scalar.activation(out=half_sin, in_=phase, func=ACT.Sin, scale=math.pi)
+        twice_sq = prodp.tile([P, 1024], F32, name="twice_sq", tag="prod")
+        nc.scalar.activation(out=twice_sq, in_=half_sin, func=ACT.Square, scale=math.sqrt(2.0))
+
+        def finish_table():
+            nc.vector.tensor_scalar(out=tab[:, 0:1024], in0=twice_sq, scalar1=-1.0, scalar2=1.0,
+                                    op0=ALU.mult, op1=ALU.add)
+            nc.vector.tensor_scalar_add(out=tab[:, 1024:1536], in0=twice_sq[:, 512:1024], scalar1=-1.0)
+            nc.vector.tensor_scalar(out=tab[:, 1536:2048], in0=twice_sq[:, 0:512], scalar1=-1.0,
+                                    scalar2=1.0, op0=ALU.mult, op1=ALU.add)
+
+        tab_v = tab.rearrange("p (a b q) -> p a q b", a=2, b=2)
+
+        def transpose_rows(src_w, col0):
+            bank = tps.tile([P, 512], F32, name="tbank")
+            for q in range(4):
+                nc.tensor.transpose(out=bank[:, P * q : P * q + P],
+                                    in_=src_w[:, col0 + P * q : col0 + P * q + P], identity=ident)
+            return bank
+
+        def regroup(eng, dst, bank):
+            src = bank.rearrange("p (g u r) -> p g r u", g=2, u=2)
+            if eng == "s":
+                nc.scalar.copy(out=dst, in_=src)
+            else:
+                nc.vector.tensor_copy(out=dst, in_=src)
+
+        def prep_x(j, eng):
+            bank = transpose_rows(xs_w, 512 * j)
+            regroup(eng, gx_w[:, 512 * j : 512 * j + 512].rearrange("p (g r u) -> p g r u", g=2, u=2), bank)
+
+        def quant_x(j0, j1):
+            nc.vector.quantize_mx(out=cx[:, 256 * j0 : 256 * j1].bitcast(FP8X4),
+                                  scales=sx[:, 256 * j0 : 256 * j1], in_=gx[:, 1024 * j0 : 1024 * j1])
+
+        gws = {}
+
+        def prep_w(g, js, engs):
+            if g not in gws:
+                gws[g] = gwp.tile([P, 4096], BF16, name="gw", align_bytes=64)
+            dst4 = gws[g].bitcast(F32).rearrange("p (g n u) -> p g n u", g=2, u=2)
+            src_w = ws[g].bitcast(F32)
+            banks = [transpose_rows(src_w, 512 * j) for j in js]
+            for j, eng, bank in zip(js, engs, banks):
+                regroup(eng, dst4[:, :, P * j : P * j + P, :], bank)
+
+        def quant_w(g, pieces):
+            n = 4096 // pieces
+            for i in range(pieces):
+                nc.vector.quantize_mx(out=cw[g][:, (n // 4) * i : (n // 4) * (i + 1)].bitcast(FP8X4),
+                                      scales=sw[g][:, (n // 4) * i : (n // 4) * (i + 1)],
+                                      in_=gws[g][:, n * i : n * (i + 1)])
+
+        def project(pool, m, g):
+            acc = pool.tile([P, 512], F32, name="acc")
+            for h in range(2):
+                c0 = 256 * m + P * h
+                nc.tensor.matmul_mx(out=acc,
+                                    lhsT=cx[:, c0 : c0 + P].bitcast(FP8X4), lhsT_scale=sx[:, c0 : c0 + P],
+                                    rhs=cw[g][:, 512 * h : 512 * h + 512].bitcast(FP8X4),
+                                    rhs_scale=sw[g][:, 512 * h : 512 * h + 512],
+                                    start=(h == 0), stop=(h == 1))
+            return acc
+
+        ys = {}
+
+        def rotate(m, g, acc):
+            half = g % 2
+            prod = prodp.tile([P, 1024], F32, name="prod", tag="prod")
+            nc.vector.tensor_tensor(
+                out=prod.rearrange("p (a q b) -> p a q b", a=2, b=2),
+                in0=acc.rearrange("p (q a) -> p a q", a=2).unsqueeze(3).to_broadcast([P, 2, 256, 2]),
+                in1=tab_v[:, :, 256 * half : 256 * half + 256, :],
+                op=ALU.mult,
+            )
+            key = (m, g // 2)
+            if key not in ys:
+                ys[key] = yp.tile([P, 1024], F32, name="y")
+            y = ys[key]
+            nc.gpsimd.tensor_tensor(out=y[:, 512 * half : 512 * half + 512], in0=prod[:, 0:512],
+                                    in1=prod[:, 512:1024], op=ALU.add)
+            if half == 1:
+                nc.sync.dma_start(out=outs[g // 2][P * m : P * m + P, :], in_=y)
+
+        vs = {}
+
+        def value(m, g):
+            half = g % 2
+            acc = project(accvp, m, g)
+            if m not in vs:
+                vs[m] = vp.tile([P, 1024], F32, name="v")
+            nc.scalar.copy(out=vs[m][:, 512 * half : 512 * half + 512], in_=acc)
+            if half == 1:
+                nc.sync.dma_start(out=outs[2][P * m : P * m + P, :], in_=vs[m])
+
+        banks = [(m, 0) for m in range(8)] + [(m, 1) for m in range(8)]
+        banks += [(m, 2 + h) for m in range(8) for h in range(2)]
+        vbanks = [(m, 4 + h) for m in range(8) for h in range(2)]
+        LOOK = 2
+        accs = {}
+
+        prep_x(0, "v")
+        prep_x(1, "v")
+        prep_w(0, [0, 1], ["s", "s"])
+        quant_x(0, 2)
+        prep_w(0, [2, 3], ["s", "v"])
+        prep_x(2, "s")
+        prep_x(3, "s")
+        quant_w(0, 2)
+        finish_table()
+        quant_x(2, 4)
+        prep_x(4, "s")
+        prep_x(5, "s")
+        for k in range(LOOK):
+            accs[k] = project(accp, banks[k][0], banks[k][1])
+
+        for k in range(32):
+            if k == 1:
+                quant_x(4, 6)
+            if k == 2:
+                quant_x(6, 8)
+            if k >= 4 and k <= 12 and k % 2 == 0:
+                quant_w((k - 2) // 2, 1)
+            if k + LOOK < 32:
+                accs[k + LOOK] = project(accp, banks[k + LOOK][0], banks[k + LOOK][1])
+            if k == 0:
+                prep_x(6, "s")
+                prep_x(7, "s")
+            if k >= 2 and k <= 10 and k % 2 == 0:
+                prep_w(k // 2, [0, 1, 2, 3], ["s", "s", "s", "s"])
+            if k >= 13 and k - 13 < 16:
+                value(vbanks[k - 13][0], vbanks[k - 13][1])
+            rotate(banks[k][0], banks[k][1], accs[k])

@@ -6,7 +6,13 @@ from concourse.masks import make_identity
 
 FLOPS = 2 * 1024 * 1024 * 3072
 
-MANUAL = False
+MANUAL = True
+WQ = {6: 1, 10: 4, 14: 2, 18: 5, 22: 3}
+LEAD = 5
+V0 = 12
+FIN1 = 5
+VADDS = (29, 31)
+LOOK = 2
 
 F32 = mybir.dt.float32
 BF16 = mybir.dt.bfloat16
@@ -29,12 +35,12 @@ def tile_attention_pa_kernel(tc, emb, W1, W2, W3, out_0, out_1, out_2):
     with ExitStack() as ctx:
         const = ctx.enter_context(tc.tile_pool(name="const", bufs=1))
         gwp = ctx.enter_context(tc.tile_pool(name="gwp", bufs=2))
-        prodp = ctx.enter_context(tc.tile_pool(name="prodp", bufs=3))
-        yp = ctx.enter_context(tc.tile_pool(name="yp", bufs=9))
-        vp = ctx.enter_context(tc.tile_pool(name="vp", bufs=3))
-        tps = ctx.enter_context(tc.psum_pool(name="tps", bufs=4))
+        prodp = ctx.enter_context(tc.tile_pool(name="prodp", bufs=4))
+        yp = ctx.enter_context(tc.tile_pool(name="yp", bufs=10))
+        vp = ctx.enter_context(tc.tile_pool(name="vp", bufs=6))
+        tps = ctx.enter_context(tc.psum_pool(name="tps", bufs=3))
         accp = ctx.enter_context(tc.psum_pool(name="accp", bufs=3))
-        accvp = ctx.enter_context(tc.psum_pool(name="accvp", bufs=1))
+        accvp = ctx.enter_context(tc.psum_pool(name="accvp", bufs=2))
         if MANUAL:
             ctx.enter_context(tc.manual_schedule())
 
@@ -50,9 +56,12 @@ def tile_attention_pa_kernel(tc, emb, W1, W2, W3, out_0, out_1, out_2):
         post = const.tile([P, 8], F32, name="post")
         freq = const.tile([P, 64], F32, name="freq")
         warm = const.tile([P, 1], F32, name="warm")
-        turns = const.tile([P, 512], F32, name="turns")
-        whole_i = const.tile([P, 512], I32, name="whole_i")
-        whole_f = const.tile([P, 512], F32, name="whole_f")
+        turns = [const.tile([P, 256], F32, name="turns%d" % h) for h in range(2)]
+        whole_i = [const.tile([P, 256], I32, name="whole_i%d" % h) for h in range(2)]
+        whole_f = [const.tile([P, 256], F32, name="whole_f%d" % h) for h in range(2)]
+        phase = [const.tile([P, 512], F32, name="phase%d" % h) for h in range(2)]
+        half_sin = [const.tile([P, 512], F32, name="half_sin%d" % h) for h in range(2)]
+        twice_sq = [const.tile([P, 512], F32, name="twice_sq%d" % h) for h in range(2)]
         tab = const.tile([P, 2048], F32, name="tab")
 
         xs_w = xs.bitcast(F32)
@@ -71,13 +80,14 @@ def tile_attention_pa_kernel(tc, emb, W1, W2, W3, out_0, out_1, out_2):
                 in_=weights[g // 2][r0 + P * j0 : r0 + P * j1, :].rearrange("(j p) k -> p j k", p=P),
             )
 
-        load_x(0, 2)
         load_w(0, 0, 2)
         load_w(0, 2, 4)
+        load_x(0, 1)
+        load_x(1, 2)
         load_x(2, 4)
         load_x(4, 6)
         load_x(6, 8)
-        for g in range(1, 6):
+        for g in (1, 4, 2, 5, 3):
             load_w(g, 0, 4)
 
         nc.vector.memset(warm, 0.0)
@@ -94,48 +104,56 @@ def tile_attention_pa_kernel(tc, emb, W1, W2, W3, out_0, out_1, out_2):
             w = 2 ** e
             nc.vector.tensor_scalar_mul(out=freq[:, w : 2 * w], in0=freq[:, 0:w], scalar1=ratio ** w)
         nc.vector.tensor_scalar_mul(out=post, in0=pos, scalar1=1.0 / (2.0 * math.pi))
-        nc.vector.tensor_tensor(
-            out=turns.rearrange("p (c i) -> p c i", c=8),
-            in0=post.unsqueeze(2).to_broadcast([P, 8, 64]),
-            in1=freq.unsqueeze(1).to_broadcast([P, 8, 64]),
-            op=ALU.mult,
-        )
-        nc.vector.tensor_scalar_add(out=whole_i, in0=turns, scalar1=0.125)
-        nc.vector.tensor_copy(out=whole_f, in_=whole_i)
-        phase = prodp.tile([P, 1024], F32, name="phase", tag="prod")
-        nc.vector.tensor_tensor(out=phase[:, 0:512], in0=turns, in1=whole_f, op=ALU.subtract)
-        nc.vector.tensor_scalar_add(out=phase[:, 512:1024], in0=phase[:, 0:512], scalar1=-0.25)
-        half_sin = prodp.tile([P, 1024], F32, name="half_sin", tag="prod")
-        nc.scalar.activation(out=half_sin, in_=phase, func=ACT.Sin, scale=math.pi)
-        twice_sq = prodp.tile([P, 1024], F32, name="twice_sq", tag="prod")
-        nc.scalar.activation(out=twice_sq, in_=half_sin, func=ACT.Square, scale=math.sqrt(2.0))
 
-        def finish_table():
-            nc.vector.tensor_scalar(out=tab[:, 0:1024], in0=twice_sq, scalar1=-1.0, scalar2=1.0,
-                                    op0=ALU.mult, op1=ALU.add)
-            nc.vector.tensor_scalar_add(out=tab[:, 1024:1536], in0=twice_sq[:, 512:1024], scalar1=-1.0)
-            nc.vector.tensor_scalar(out=tab[:, 1536:2048], in0=twice_sq[:, 0:512], scalar1=-1.0,
-                                    scalar2=1.0, op0=ALU.mult, op1=ALU.add)
-
+        tab_p = tab.rearrange("p (s q) -> p s q", s=4)
         tab_v = tab.rearrange("p (a b q) -> p a q b", a=2, b=2)
 
-        def transpose_rows(src_w, col0):
+        def table_angles(h):
+            nc.vector.tensor_tensor(
+                out=turns[h].rearrange("p (c i) -> p c i", c=4),
+                in0=post[:, 4 * h : 4 * h + 4].unsqueeze(2).to_broadcast([P, 4, 64]),
+                in1=freq.unsqueeze(1).to_broadcast([P, 4, 64]),
+                op=ALU.mult,
+            )
+            nc.vector.tensor_scalar_add(out=whole_i[h], in0=turns[h], scalar1=0.125)
+            nc.vector.tensor_copy(out=whole_f[h], in_=whole_i[h])
+            nc.vector.tensor_tensor(out=phase[h][:, 0:256], in0=turns[h], in1=whole_f[h], op=ALU.subtract)
+            nc.vector.tensor_scalar_add(out=phase[h][:, 256:512], in0=phase[h][:, 0:256], scalar1=-0.25)
+
+        def table_sines(h):
+            nc.scalar.activation(out=half_sin[h], in_=phase[h], func=ACT.Sin, scale=math.pi)
+            nc.scalar.activation(out=twice_sq[h], in_=half_sin[h], func=ACT.Square, scale=math.sqrt(2.0))
+
+        def finish_table(h):
+            q0 = 256 * h
+            nc.vector.tensor_scalar(out=tab_p[:, 0:2, q0 : q0 + 256],
+                                    in0=twice_sq[h].rearrange("p (s q) -> p s q", s=2),
+                                    scalar1=-1.0, scalar2=1.0, op0=ALU.mult, op1=ALU.add)
+            nc.vector.tensor_scalar_add(out=tab_p[:, 2, q0 : q0 + 256], in0=twice_sq[h][:, 256:512], scalar1=-1.0)
+            nc.vector.tensor_scalar(out=tab_p[:, 3, q0 : q0 + 256], in0=twice_sq[h][:, 0:256],
+                                    scalar1=-1.0, scalar2=1.0, op0=ALU.mult, op1=ALU.add)
+
+        tbanks = {}
+
+        def transpose_rows(key, src_w, col0):
             bank = tps.tile([P, 512], F32, name="tbank")
             for q in range(4):
                 nc.tensor.transpose(out=bank[:, P * q : P * q + P],
                                     in_=src_w[:, col0 + P * q : col0 + P * q + P], identity=ident)
-            return bank
+            tbanks[key] = bank
 
-        def regroup(eng, dst, bank):
-            src = bank.rearrange("p (g u r) -> p g r u", g=2, u=2)
+        def regroup(eng, dst, key):
+            src = tbanks[key].rearrange("p (g u r) -> p g r u", g=2, u=2)
             if eng == "s":
                 nc.scalar.copy(out=dst, in_=src)
             else:
                 nc.vector.tensor_copy(out=dst, in_=src)
 
-        def prep_x(j, eng):
-            bank = transpose_rows(xs_w, 512 * j)
-            regroup(eng, gx_w[:, 512 * j : 512 * j + 512].rearrange("p (g r u) -> p g r u", g=2, u=2), bank)
+        def tx(j):
+            transpose_rows(("x", j), xs_w, 512 * j)
+
+        def cpx(j, eng):
+            regroup(eng, gx_w[:, 512 * j : 512 * j + 512].rearrange("p (g r u) -> p g r u", g=2, u=2), ("x", j))
 
         def quant_x(j0, j1):
             nc.vector.quantize_mx(out=cx[:, 256 * j0 : 256 * j1].bitcast(FP8X4),
@@ -143,14 +161,14 @@ def tile_attention_pa_kernel(tc, emb, W1, W2, W3, out_0, out_1, out_2):
 
         gws = {}
 
-        def prep_w(g, js, engs):
+        def tw(g, j):
+            transpose_rows((g, j), ws[g].bitcast(F32), 512 * j)
+
+        def cpw(g, j, eng):
             if g not in gws:
                 gws[g] = gwp.tile([P, 4096], BF16, name="gw", align_bytes=64)
             dst4 = gws[g].bitcast(F32).rearrange("p (g n u) -> p g n u", g=2, u=2)
-            src_w = ws[g].bitcast(F32)
-            banks = [transpose_rows(src_w, 512 * j) for j in js]
-            for j, eng, bank in zip(js, engs, banks):
-                regroup(eng, dst4[:, :, P * j : P * j + P, :], bank)
+            regroup(eng, dst4[:, :, P * j : P * j + P, :], (g, j))
 
         def quant_w(g, pieces):
             n = 4096 // pieces
@@ -170,72 +188,92 @@ def tile_attention_pa_kernel(tc, emb, W1, W2, W3, out_0, out_1, out_2):
                                     start=(h == 0), stop=(h == 1))
             return acc
 
-        ys = {}
-
-        def rotate(m, g, acc):
+        def rotate(k, m, g, acc):
             half = g % 2
-            prod = prodp.tile([P, 1024], F32, name="prod", tag="prod")
+            prod = prodp.tile([P, 1024], F32, name="prod")
             nc.vector.tensor_tensor(
                 out=prod.rearrange("p (a q b) -> p a q b", a=2, b=2),
                 in0=acc.rearrange("p (q a) -> p a q", a=2).unsqueeze(3).to_broadcast([P, 2, 256, 2]),
                 in1=tab_v[:, :, 256 * half : 256 * half + 256, :],
                 op=ALU.mult,
             )
-            key = (m, g // 2)
-            if key not in ys:
-                ys[key] = yp.tile([P, 1024], F32, name="y")
-            y = ys[key]
-            nc.gpsimd.tensor_tensor(out=y[:, 512 * half : 512 * half + 512], in0=prod[:, 0:512],
-                                    in1=prod[:, 512:1024], op=ALU.add)
-            if half == 1:
-                nc.sync.dma_start(out=outs[g // 2][P * m : P * m + P, :], in_=y)
+            y = yp.tile([P, 512], F32, name="y")
+            if k in VADDS:
+                nc.vector.tensor_tensor(out=y, in0=prod[:, 0:512], in1=prod[:, 512:1024], op=ALU.add)
+            else:
+                nc.gpsimd.tensor_tensor(out=y, in0=prod[:, 0:512], in1=prod[:, 512:1024], op=ALU.add)
+            nc.sync.dma_start(out=outs[g // 2][P * m : P * m + P, 512 * half : 512 * half + 512], in_=y)
 
-        vs = {}
+        vaccs = {}
 
-        def value(m, g):
-            half = g % 2
-            acc = project(accvp, m, g)
-            if m not in vs:
-                vs[m] = vp.tile([P, 1024], F32, name="v")
-            nc.scalar.copy(out=vs[m][:, 512 * half : 512 * half + 512], in_=acc)
-            if half == 1:
-                nc.sync.dma_start(out=outs[2][P * m : P * m + P, :], in_=vs[m])
+        def value_mm(i):
+            vaccs[i] = project(accvp, i % 8, 4 + i // 8)
 
-        banks = [(m, 0) for m in range(8)] + [(m, 1) for m in range(8)]
-        banks += [(m, 2 + h) for m in range(8) for h in range(2)]
-        vbanks = [(m, 4 + h) for m in range(8) for h in range(2)]
-        LOOK = 2
+        def value_out(i):
+            m = i % 8
+            half = i // 8
+            v = vp.tile([P, 512], F32, name="v")
+            nc.scalar.copy(out=v, in_=vaccs[i])
+            nc.sync.dma_start(out=outs[2][P * m : P * m + P, 512 * half : 512 * half + 512], in_=v)
+
+        banks = [(m, g) for g in range(4) for m in range(8)]
         accs = {}
 
-        prep_x(0, "v")
-        prep_x(1, "v")
-        prep_w(0, [0, 1], ["s", "s"])
-        quant_x(0, 2)
-        prep_w(0, [2, 3], ["s", "v"])
-        prep_x(2, "s")
-        prep_x(3, "s")
+        table_angles(0)
+        table_sines(0)
+        table_angles(1)
+        for j in range(4):
+            tw(0, j)
+        cpw(0, 0, "s")
+        cpw(0, 1, "v")
+        cpw(0, 2, "s")
+        cpw(0, 3, "v")
+        tx(0)
+        tx(1)
+        cpx(0, "s")
+        cpx(1, "s")
         quant_w(0, 2)
-        finish_table()
+        quant_x(0, 1)
+        tx(2)
+        tx(3)
+        cpx(2, "s")
+        cpx(3, "s")
+        accs[0] = project(accp, 0, 0)
+        quant_x(1, 2)
+        finish_table(0)
+        tx(4)
+        tx(5)
+        accs[1] = project(accp, 1, 0)
+        cpx(4, "s")
+        cpx(5, "s")
         quant_x(2, 4)
-        prep_x(4, "s")
-        prep_x(5, "s")
-        for k in range(LOOK):
-            accs[k] = project(accp, banks[k][0], banks[k][1])
 
         for k in range(32):
             if k == 1:
                 quant_x(4, 6)
-            if k == 2:
+            if k == 3:
                 quant_x(6, 8)
-            if k >= 4 and k <= 12 and k % 2 == 0:
-                quant_w((k - 2) // 2, 1)
+            if k == FIN1:
+                finish_table(1)
+            if k in WQ:
+                quant_w(WQ[k], 1)
             if k + LOOK < 32:
                 accs[k + LOOK] = project(accp, banks[k + LOOK][0], banks[k + LOOK][1])
+            if k >= V0 and k - V0 < 16:
+                value_mm(k - V0)
             if k == 0:
-                prep_x(6, "s")
-                prep_x(7, "s")
-            if k >= 2 and k <= 10 and k % 2 == 0:
-                prep_w(k // 2, [0, 1, 2, 3], ["s", "s", "s", "s"])
-            if k >= 13 and k - 13 < 16:
-                value(vbanks[k - 13][0], vbanks[k - 13][1])
-            rotate(banks[k][0], banks[k][1], accs[k])
+                tx(6)
+                tx(7)
+                cpx(6, "s")
+                cpx(7, "s")
+            if k == 2:
+                table_sines(1)
+            for d, js in ((LEAD, (0, 1)), (LEAD - 1, (2, 3))):
+                if k + d in WQ:
+                    for j in js:
+                        tw(WQ[k + d], j)
+                    for j in js:
+                        cpw(WQ[k + d], j, "s")
+            if k >= V0 and k - V0 < 16:
+                value_out(k - V0)
+            rotate(k, banks[k][0], banks[k][1], accs[k])

@@ -6,7 +6,7 @@ from concourse.masks import make_identity
 
 FLOPS = 2 * 1024 * 1024 * 3072
 
-MANUAL = True
+MANUAL = False
 WQ = {6: 1, 10: 4, 14: 2, 18: 5, 22: 3}
 LEAD = 5
 V0 = 12

@@ -13,6 +13,8 @@ V0 = 12
 FIN1 = 5
 VADDS = (29, 31)
 LOOK = 2
+PAIRED = 28
+FIN1_ACT = True
 
 F32 = mybir.dt.float32
 BF16 = mybir.dt.bfloat16
@@ -35,8 +37,8 @@ def tile_attention_pa_kernel(tc, emb, W1, W2, W3, out_0, out_1, out_2):
     with ExitStack() as ctx:
         const = ctx.enter_context(tc.tile_pool(name="const", bufs=1))
         gwp = ctx.enter_context(tc.tile_pool(name="gwp", bufs=2))
-        prodp = ctx.enter_context(tc.tile_pool(name="prodp", bufs=4))
-        yp = ctx.enter_context(tc.tile_pool(name="yp", bufs=10))
+        prodp = ctx.enter_context(tc.tile_pool(name="prodp", bufs=3))
+        yp = ctx.enter_context(tc.tile_pool(name="yp", bufs=6))
         vp = ctx.enter_context(tc.tile_pool(name="vp", bufs=6))
         tps = ctx.enter_context(tc.psum_pool(name="tps", bufs=3))
         accp = ctx.enter_context(tc.psum_pool(name="accp", bufs=3))
@@ -133,6 +135,16 @@ def tile_attention_pa_kernel(tc, emb, W1, W2, W3, out_0, out_1, out_2):
             nc.vector.tensor_scalar(out=tab_p[:, 3, q0 : q0 + 256], in0=twice_sq[h][:, 0:256],
                                     scalar1=-1.0, scalar2=1.0, op0=ALU.mult, op1=ALU.add)
 
+        def finish_table_act(h):
+            q0 = 256 * h
+            nc.scalar.activation(out=tab_p[:, 0:2, q0 : q0 + 256],
+                                 in_=twice_sq[h].rearrange("p (s q) -> p s q", s=2),
+                                 func=ACT.Copy, scale=-1.0, bias=1.0)
+            nc.scalar.activation(out=tab_p[:, 2, q0 : q0 + 256], in_=twice_sq[h][:, 256:512],
+                                 func=ACT.Copy, scale=1.0, bias=-1.0)
+            nc.scalar.activation(out=tab_p[:, 3, q0 : q0 + 256], in_=twice_sq[h][:, 0:256],
+                                 func=ACT.Copy, scale=-1.0, bias=1.0)
+
         tbanks = {}
 
         def transpose_rows(key, src_w, col0):
@@ -188,16 +200,33 @@ def tile_attention_pa_kernel(tc, emb, W1, W2, W3, out_0, out_1, out_2):
                                     start=(h == 0), stop=(h == 1))
             return acc
 
+        pair = {}
+
         def rotate(k, m, g, acc):
             half = g % 2
-            prod = prodp.tile([P, 1024], F32, name="prod")
+            if k < PAIRED:
+                if k % 2 == 0:
+                    pair["prod"] = prodp.tile([P, 2048], F32, name="prod2")
+                prod = pair["prod"][:, 1024 * (k % 2) : 1024 * (k % 2) + 1024]
+            else:
+                prod = prodp.tile([P, 1024], F32, name="prod", tag="prod2")
             nc.vector.tensor_tensor(
                 out=prod.rearrange("p (a q b) -> p a q b", a=2, b=2),
                 in0=acc.rearrange("p (q a) -> p a q", a=2).unsqueeze(3).to_broadcast([P, 2, 256, 2]),
                 in1=tab_v[:, :, 256 * half : 256 * half + 256, :],
                 op=ALU.mult,
             )
-            y = yp.tile([P, 512], F32, name="y")
+            if k < PAIRED:
+                if k % 2 == 1:
+                    both = pair["prod"].rearrange("p (j a n) -> p j a n", j=2, a=2)
+                    y2 = yp.tile([P, 2, 512], F32, name="y2")
+                    nc.gpsimd.tensor_tensor(out=y2, in0=both[:, :, 0, :], in1=both[:, :, 1, :], op=ALU.add)
+                    nc.sync.dma_start(
+                        out=outs[g // 2][P * (m - 1) : P * (m + 1), 512 * half : 512 * half + 512].rearrange(
+                            "(j p) n -> p j n", p=P),
+                        in_=y2)
+                return
+            y = yp.tile([P, 512], F32, name="y", tag="y2")
             if k in VADDS:
                 nc.vector.tensor_tensor(out=y, in0=prod[:, 0:512], in1=prod[:, 512:1024], op=ALU.add)
             else:
@@ -253,7 +282,7 @@ def tile_attention_pa_kernel(tc, emb, W1, W2, W3, out_0, out_1, out_2):
                 quant_x(4, 6)
             if k == 3:
                 quant_x(6, 8)
-            if k == FIN1:
+            if k == FIN1 and not FIN1_ACT:
                 finish_table(1)
             if k in WQ:
                 quant_w(WQ[k], 1)
@@ -268,6 +297,8 @@ def tile_attention_pa_kernel(tc, emb, W1, W2, W3, out_0, out_1, out_2):
                 cpx(7, "s")
             if k == 2:
                 table_sines(1)
+                if FIN1_ACT:
+                    finish_table_act(1)
             for d, js in ((LEAD, (0, 1)), (LEAD - 1, (2, 3))):
                 if k + d in WQ:
                     for j in js:

@@ -13,6 +13,7 @@ V0 = 12
 FIN1 = 5
 VADDS = (29, 31)
 LOOK = 2
+FIRST_PAIR = 2
 PAIRED = 28
 FIN1_ACT = True
 
@@ -82,9 +83,9 @@ def tile_attention_pa_kernel(tc, emb, W1, W2, W3, out_0, out_1, out_2):
                 in_=weights[g // 2][r0 + P * j0 : r0 + P * j1, :].rearrange("(j p) k -> p j k", p=P),
             )
 
+        load_x(0, 1)
         load_w(0, 0, 2)
         load_w(0, 2, 4)
-        load_x(0, 1)
         load_x(1, 2)
         load_x(2, 4)
         load_x(4, 6)
@@ -189,6 +190,20 @@ def tile_attention_pa_kernel(tc, emb, W1, W2, W3, out_0, out_1, out_2):
                                       scales=sw[g][:, (n // 4) * i : (n // 4) * (i + 1)],
                                       in_=gws[g][:, n * i : n * (i + 1)])
 
+        def quant_w0(f):
+            for h in range(2):
+                c0 = 512 * h + 256 * f
+                nc.vector.quantize_mx(out=cw[0][:, c0 : c0 + 256].bitcast(FP8X4), scales=sw[0][:, c0 : c0 + 256],
+                                      in_=gws[0][:, 4 * c0 : 4 * c0 + 1024])
+
+        def project0(acc, f):
+            for h in range(2):
+                c0 = 512 * h + 256 * f
+                nc.tensor.matmul_mx(out=acc,
+                                    lhsT=cx[:, P * h : P * h + P].bitcast(FP8X4), lhsT_scale=sx[:, P * h : P * h + P],
+                                    rhs=cw[0][:, c0 : c0 + 256].bitcast(FP8X4), rhs_scale=sw[0][:, c0 : c0 + 256],
+                                    start=(h == 0), stop=(h == 1))
+
         def project(pool, m, g):
             acc = pool.tile([P, 512], F32, name="acc")
             for h in range(2):
@@ -204,19 +219,22 @@ def tile_attention_pa_kernel(tc, emb, W1, W2, W3, out_0, out_1, out_2):
 
         def rotate(k, m, g, acc):
             half = g % 2
-            if k < PAIRED:
+            if FIRST_PAIR <= k < PAIRED:
                 if k % 2 == 0:
                     pair["prod"] = prodp.tile([P, 2048], F32, name="prod2")
                 prod = pair["prod"][:, 1024 * (k % 2) : 1024 * (k % 2) + 1024]
             else:
                 prod = prodp.tile([P, 1024], F32, name="prod", tag="prod2")
-            nc.vector.tensor_tensor(
-                out=prod.rearrange("p (a q b) -> p a q b", a=2, b=2),
-                in0=acc.rearrange("p (q a) -> p a q", a=2).unsqueeze(3).to_broadcast([P, 2, 256, 2]),
-                in1=tab_v[:, :, 256 * half : 256 * half + 256, :],
-                op=ALU.mult,
-            )
-            if k < PAIRED:
+            pieces = 2 if k == 0 else 1
+            n = 256 // pieces
+            for f in range(pieces):
+                nc.vector.tensor_tensor(
+                    out=prod.rearrange("p (a q b) -> p a q b", a=2, b=2)[:, :, n * f : n * f + n, :],
+                    in0=(acc[f] if k == 0 else acc).rearrange("p (q a) -> p a q", a=2).unsqueeze(3).to_broadcast([P, 2, n, 2]),
+                    in1=tab_v[:, :, 256 * half + n * f : 256 * half + n * f + n, :],
+                    op=ALU.mult,
+                )
+            if FIRST_PAIR <= k < PAIRED:
                 if k % 2 == 1:
                     both = pair["prod"].rearrange("p (j a n) -> p j a n", j=2, a=2)
                     y2 = yp.tile([P, 2, 512], F32, name="y2")
@@ -251,37 +269,45 @@ def tile_attention_pa_kernel(tc, emb, W1, W2, W3, out_0, out_1, out_2):
         table_angles(0)
         table_sines(0)
         table_angles(1)
-        for j in range(4):
-            tw(0, j)
+        tx(0)
+        cpx(0, "v")
+        tw(0, 0)
+        tw(0, 1)
         cpw(0, 0, "s")
         cpw(0, 1, "v")
+        quant_x(0, 1)
+        finish_table(0)
+        quant_w0(0)
+        acc0 = [accp.tile([P, 256], F32, name="acc") for f in range(2)]
+        accs[0] = acc0
+        tw(0, 2)
+        tw(0, 3)
+        project0(acc0[0], 0)
         cpw(0, 2, "s")
         cpw(0, 3, "v")
-        tx(0)
+        quant_w0(1)
         tx(1)
-        cpx(0, "s")
+        project0(acc0[1], 1)
         cpx(1, "s")
-        quant_w(0, 2)
-        quant_x(0, 1)
         tx(2)
         tx(3)
         cpx(2, "s")
         cpx(3, "s")
-        accs[0] = project(accp, 0, 0)
         quant_x(1, 2)
-        finish_table(0)
         tx(4)
         tx(5)
         accs[1] = project(accp, 1, 0)
         cpx(4, "s")
         cpx(5, "s")
         quant_x(2, 4)
+        tx(6)
+        tx(7)
+        cpx(6, "s")
+        cpx(7, "s")
 
         for k in range(32):
             if k == 1:
-                quant_x(4, 6)
-            if k == 3:
-                quant_x(6, 8)
+                quant_x(4, 8)
             if k == FIN1 and not FIN1_ACT:
                 finish_table(1)
             if k in WQ:
@@ -290,11 +316,6 @@ def tile_attention_pa_kernel(tc, emb, W1, W2, W3, out_0, out_1, out_2):
                 accs[k + LOOK] = project(accp, banks[k + LOOK][0], banks[k + LOOK][1])
             if k >= V0 and k - V0 < 16:
                 value_mm(k - V0)
-            if k == 0:
-                tx(6)
-                tx(7)
-                cpx(6, "s")
-                cpx(7, "s")
             if k == 2:
                 table_sines(1)
                 if FIN1_ACT:

@@ -7,7 +7,7 @@ from concourse.masks import make_identity
 FLOPS = 2 * 1024 * 1024 * 3072
 
 MANUAL = False
-WQ = {6: 1, 10: 4, 14: 2, 18: 5, 22: 3}
+WQ = {6: 1, 9: 4, 11: 5, 14: 2, 22: 3}
 LEAD = 5
 V0 = 12
 FIN1 = 5
@@ -40,7 +40,7 @@ def tile_attention_pa_kernel(tc, emb, W1, W2, W3, out_0, out_1, out_2):
         gwp = ctx.enter_context(tc.tile_pool(name="gwp", bufs=2))
         prodp = ctx.enter_context(tc.tile_pool(name="prodp", bufs=3))
         yp = ctx.enter_context(tc.tile_pool(name="yp", bufs=6))
-        vp = ctx.enter_context(tc.tile_pool(name="vp", bufs=6))
+        vp = ctx.enter_context(tc.tile_pool(name="vp", bufs=4))
         tps = ctx.enter_context(tc.psum_pool(name="tps", bufs=3))
         accp = ctx.enter_context(tc.psum_pool(name="accp", bufs=3))
         accvp = ctx.enter_context(tc.psum_pool(name="accvp", bufs=2))
@@ -90,7 +90,7 @@ def tile_attention_pa_kernel(tc, emb, W1, W2, W3, out_0, out_1, out_2):
         load_x(2, 4)
         load_x(4, 6)
         load_x(6, 8)
-        for g in (1, 4, 2, 5, 3):
+        for g in (1, 4, 5, 2, 3):
             load_w(g, 0, 4)
 
         nc.vector.memset(warm, 0.0)
@@ -254,14 +254,16 @@ def tile_attention_pa_kernel(tc, emb, W1, W2, W3, out_0, out_1, out_2):
         vaccs = {}
 
         def value_mm(i):
-            vaccs[i] = project(accvp, i % 8, 4 + i // 8)
+            vaccs[i] = project(accvp, i // 2, 4 + i % 2)
 
         def value_out(i):
-            m = i % 8
-            half = i // 8
-            v = vp.tile([P, 512], F32, name="v")
-            nc.scalar.copy(out=v, in_=vaccs[i])
-            nc.sync.dma_start(out=outs[2][P * m : P * m + P, 512 * half : 512 * half + 512], in_=v)
+            m = i // 2
+            half = i % 2
+            if half == 0:
+                pair["v"] = vp.tile([P, 1024], F32, name="v")
+            nc.scalar.copy(out=pair["v"][:, 512 * half : 512 * half + 512], in_=vaccs[i])
+            if half == 1:
+                nc.sync.dma_start(out=outs[2][P * m : P * m + P, :], in_=pair["v"])
 
         banks = [(m, g) for g in range(4) for m in range(8)]
         accs = {}

import math
from contextlib import ExitStack

import concourse.mybir as mybir
from concourse.masks import make_identity

FLOPS = 2 * 1024 * 1024 * 3072

MANUAL = False
WQ = {6: 1, 9: 4, 11: 5, 14: 2, 22: 3}
LEAD = 5
V0 = 12
FIN1 = 5
VADDS = (29, 31)
LOOK = 2
FIRST_PAIR = 2
PAIRED = 28
FIN1_ACT = True

F32 = mybir.dt.float32
BF16 = mybir.dt.bfloat16
I32 = mybir.dt.int32
U32 = mybir.dt.uint32
U8 = mybir.dt.uint8
FP8X4 = mybir.dt.float8_e4m3fn_x4
ALU = mybir.AluOpType
ACT = mybir.ActivationFunctionType

P = 128


def tile_attention_pa_kernel(tc, emb, W1, W2, W3, out_0, out_1, out_2):
    nc = tc.nc
    x2d = emb.flatten_outer_dims()
    weights = [W1, W2, W3]
    outs = [o.rearrange("b h (a c) d -> (b h a) (c d)", c=8) for o in (out_0, out_1, out_2)]

    with ExitStack() as ctx:
        const = ctx.enter_context(tc.tile_pool(name="const", bufs=1))
        gwp = ctx.enter_context(tc.tile_pool(name="gwp", bufs=2))
        prodp = ctx.enter_context(tc.tile_pool(name="prodp", bufs=3))
        yp = ctx.enter_context(tc.tile_pool(name="yp", bufs=6))
        vp = ctx.enter_context(tc.tile_pool(name="vp", bufs=4))
        tps = ctx.enter_context(tc.psum_pool(name="tps", bufs=3))
        accp = ctx.enter_context(tc.psum_pool(name="accp", bufs=3))
        accvp = ctx.enter_context(tc.psum_pool(name="accvp", bufs=2))
        if MANUAL:
            ctx.enter_context(tc.manual_schedule())

        xs = const.tile([P, 8192], BF16, name="xs")
        ws = [const.tile([P, 4096], BF16, name="ws%d" % g) for g in range(6)]
        gx = const.tile([P, 8192], BF16, name="gx", align_bytes=64)
        cx = const.tile([P, 2048], U32, name="cx", align_bytes=64)
        sx = const.tile([P, 2048], U8, name="sx", align_bytes=64)
        cw = [const.tile([P, 1024], U32, name="cw%d" % g, align_bytes=64) for g in range(6)]
        sw = [const.tile([P, 1024], U8, name="sw%d" % g, align_bytes=64) for g in range(6)]
        ident = const.tile([P, P], F32, name="ident")
        pos = const.tile([P, 8], F32, name="pos")
        post = const.tile([P, 8], F32, name="post")
        freq = const.tile([P, 64], F32, name="freq")
        warm = const.tile([P, 1], F32, name="warm")
        turns = [const.tile([P, 256], F32, name="turns%d" % h) for h in range(2)]
        whole_i = [const.tile([P, 256], I32, name="whole_i%d" % h) for h in range(2)]
        whole_f = [const.tile([P, 256], F32, name="whole_f%d" % h) for h in range(2)]
        phase = [const.tile([P, 512], F32, name="phase%d" % h) for h in range(2)]
        half_sin = [const.tile([P, 512], F32, name="half_sin%d" % h) for h in range(2)]
        twice_sq = [const.tile([P, 512], F32, name="twice_sq%d" % h) for h in range(2)]
        tab = const.tile([P, 2048], F32, name="tab")

        xs_w = xs.bitcast(F32)
        gx_w = gx.bitcast(F32)

        def load_x(j0, j1):
            nc.sync.dma_start(
                out=xs[:, 1024 * j0 : 1024 * j1].rearrange("p (j k) -> p j k", k=1024),
                in_=x2d[P * j0 : P * j1, :].rearrange("(j p) k -> p j k", p=P),
            )

        def load_w(g, j0, j1):
            r0 = 512 * (g % 2)
            nc.sync.dma_start(
                out=ws[g][:, 1024 * j0 : 1024 * j1].rearrange("p (j k) -> p j k", k=1024),
                in_=weights[g // 2][r0 + P * j0 : r0 + P * j1, :].rearrange("(j p) k -> p j k", p=P),
            )

        load_x(0, 1)
        load_w(0, 0, 2)
        load_w(0, 2, 4)
        load_x(1, 2)
        load_x(2, 4)
        load_x(4, 6)
        load_x(6, 8)
        for g in (1, 4, 5, 2, 3):
            load_w(g, 0, 4)

        nc.vector.memset(warm, 0.0)
        nc.scalar.activation(out=warm, in_=warm, func=ACT.Sin)
        nc.gpsimd.iota(pos[0:64, :], pattern=[[1, 8]], base=0, channel_multiplier=8,
                       allow_small_or_imprecise_dtypes=True)
        nc.gpsimd.iota(pos[64:128, :], pattern=[[1, 8]], base=0, channel_multiplier=8,
                       allow_small_or_imprecise_dtypes=True)
        make_identity(nc, ident)

        ratio = 10000.0 ** (-1.0 / 64.0)
        nc.vector.memset(freq[:, 0:1], 1.0)
        for e in range(6):
            w = 2 ** e
            nc.vector.tensor_scalar_mul(out=freq[:, w : 2 * w], in0=freq[:, 0:w], scalar1=ratio ** w)
        nc.vector.tensor_scalar_mul(out=post, in0=pos, scalar1=1.0 / (2.0 * math.pi))

        tab_p = tab.rearrange("p (s q) -> p s q", s=4)
        tab_v = tab.rearrange("p (a b q) -> p a q b", a=2, b=2)

        def table_angles(h):
            nc.vector.tensor_tensor(
                out=turns[h].rearrange("p (c i) -> p c i", c=4),
                in0=post[:, 4 * h : 4 * h + 4].unsqueeze(2).to_broadcast([P, 4, 64]),
                in1=freq.unsqueeze(1).to_broadcast([P, 4, 64]),
                op=ALU.mult,
            )
            nc.vector.tensor_scalar_add(out=whole_i[h], in0=turns[h], scalar1=0.125)
            nc.vector.tensor_copy(out=whole_f[h], in_=whole_i[h])
            nc.vector.tensor_tensor(out=phase[h][:, 0:256], in0=turns[h], in1=whole_f[h], op=ALU.subtract)
            nc.vector.tensor_scalar_add(out=phase[h][:, 256:512], in0=phase[h][:, 0:256], scalar1=-0.25)

        def table_sines(h):
            nc.scalar.activation(out=half_sin[h], in_=phase[h], func=ACT.Sin, scale=math.pi)
            nc.scalar.activation(out=twice_sq[h], in_=half_sin[h], func=ACT.Square, scale=math.sqrt(2.0))

        def finish_table(h):
            q0 = 256 * h
            nc.vector.tensor_scalar(out=tab_p[:, 0:2, q0 : q0 + 256],
                                    in0=twice_sq[h].rearrange("p (s q) -> p s q", s=2),
                                    scalar1=-1.0, scalar2=1.0, op0=ALU.mult, op1=ALU.add)
            nc.vector.tensor_scalar_add(out=tab_p[:, 2, q0 : q0 + 256], in0=twice_sq[h][:, 256:512], scalar1=-1.0)
            nc.vector.tensor_scalar(out=tab_p[:, 3, q0 : q0 + 256], in0=twice_sq[h][:, 0:256],
                                    scalar1=-1.0, scalar2=1.0, op0=ALU.mult, op1=ALU.add)

        def finish_table_act(h):
            q0 = 256 * h
            nc.scalar.activation(out=tab_p[:, 0:2, q0 : q0 + 256],
                                 in_=twice_sq[h].rearrange("p (s q) -> p s q", s=2),
                                 func=ACT.Copy, scale=-1.0, bias=1.0)
            nc.scalar.activation(out=tab_p[:, 2, q0 : q0 + 256], in_=twice_sq[h][:, 256:512],
                                 func=ACT.Copy, scale=1.0, bias=-1.0)
            nc.scalar.activation(out=tab_p[:, 3, q0 : q0 + 256], in_=twice_sq[h][:, 0:256],
                                 func=ACT.Copy, scale=-1.0, bias=1.0)

        tbanks = {}

        def transpose_rows(key, src_w, col0):
            bank = tps.tile([P, 512], F32, name="tbank")
            for q in range(4):
                nc.tensor.transpose(out=bank[:, P * q : P * q + P],
                                    in_=src_w[:, col0 + P * q : col0 + P * q + P], identity=ident)
            tbanks[key] = bank

        def regroup(eng, dst, key):
            src = tbanks[key].rearrange("p (g u r) -> p g r u", g=2, u=2)
            if eng == "s":
                nc.scalar.copy(out=dst, in_=src)
            else:
                nc.vector.tensor_copy(out=dst, in_=src)

        def tx(j):
            transpose_rows(("x", j), xs_w, 512 * j)

        def cpx(j, eng):
            regroup(eng, gx_w[:, 512 * j : 512 * j + 512].rearrange("p (g r u) -> p g r u", g=2, u=2), ("x", j))

        def quant_x(j0, j1):
            nc.vector.quantize_mx(out=cx[:, 256 * j0 : 256 * j1].bitcast(FP8X4),
                                  scales=sx[:, 256 * j0 : 256 * j1], in_=gx[:, 1024 * j0 : 1024 * j1])

        gws = {}

        def tw(g, j):
            transpose_rows((g, j), ws[g].bitcast(F32), 512 * j)

        def cpw(g, j, eng):
            if g not in gws:
                gws[g] = gwp.tile([P, 4096], BF16, name="gw", align_bytes=64)
            dst4 = gws[g].bitcast(F32).rearrange("p (g n u) -> p g n u", g=2, u=2)
            regroup(eng, dst4[:, :, P * j : P * j + P, :], (g, j))

        def quant_w(g, pieces):
            n = 4096 // pieces
            for i in range(pieces):
                nc.vector.quantize_mx(out=cw[g][:, (n // 4) * i : (n // 4) * (i + 1)].bitcast(FP8X4),
                                      scales=sw[g][:, (n // 4) * i : (n // 4) * (i + 1)],
                                      in_=gws[g][:, n * i : n * (i + 1)])

        def quant_w0(f):
            for h in range(2):
                c0 = 512 * h + 256 * f
                nc.vector.quantize_mx(out=cw[0][:, c0 : c0 + 256].bitcast(FP8X4), scales=sw[0][:, c0 : c0 + 256],
                                      in_=gws[0][:, 4 * c0 : 4 * c0 + 1024])

        def project0(acc, f):
            for h in range(2):
                c0 = 512 * h + 256 * f
                nc.tensor.matmul_mx(out=acc,
                                    lhsT=cx[:, P * h : P * h + P].bitcast(FP8X4), lhsT_scale=sx[:, P * h : P * h + P],
                                    rhs=cw[0][:, c0 : c0 + 256].bitcast(FP8X4), rhs_scale=sw[0][:, c0 : c0 + 256],
                                    start=(h == 0), stop=(h == 1))

        def project(pool, m, g):
            acc = pool.tile([P, 512], F32, name="acc")
            for h in range(2):
                c0 = 256 * m + P * h
                nc.tensor.matmul_mx(out=acc,
                                    lhsT=cx[:, c0 : c0 + P].bitcast(FP8X4), lhsT_scale=sx[:, c0 : c0 + P],
                                    rhs=cw[g][:, 512 * h : 512 * h + 512].bitcast(FP8X4),
                                    rhs_scale=sw[g][:, 512 * h : 512 * h + 512],
                                    start=(h == 0), stop=(h == 1))
            return acc

        pair = {}

        def rotate(k, m, g, acc):
            half = g % 2
            if FIRST_PAIR <= k < PAIRED:
                if k % 2 == 0:
                    pair["prod"] = prodp.tile([P, 2048], F32, name="prod2")
                prod = pair["prod"][:, 1024 * (k % 2) : 1024 * (k % 2) + 1024]
            else:
                prod = prodp.tile([P, 1024], F32, name="prod", tag="prod2")
            pieces = 2 if k == 0 else 1
            n = 256 // pieces
            for f in range(pieces):
                nc.vector.tensor_tensor(
                    out=prod.rearrange("p (a q b) -> p a q b", a=2, b=2)[:, :, n * f : n * f + n, :],
                    in0=(acc[f] if k == 0 else acc).rearrange("p (q a) -> p a q", a=2).unsqueeze(3).to_broadcast([P, 2, n, 2]),
                    in1=tab_v[:, :, 256 * half + n * f : 256 * half + n * f + n, :],
                    op=ALU.mult,
                )
            if FIRST_PAIR <= k < PAIRED:
                if k % 2 == 1:
                    both = pair["prod"].rearrange("p (j a n) -> p j a n", j=2, a=2)
                    y2 = yp.tile([P, 2, 512], F32, name="y2")
                    nc.gpsimd.tensor_tensor(out=y2, in0=both[:, :, 0, :], in1=both[:, :, 1, :], op=ALU.add)
                    nc.sync.dma_start(
                        out=outs[g // 2][P * (m - 1) : P * (m + 1), 512 * half : 512 * half + 512].rearrange(
                            "(j p) n -> p j n", p=P),
                        in_=y2)
                return
            y = yp.tile([P, 512], F32, name="y", tag="y2")
            if k in VADDS:
                nc.vector.tensor_tensor(out=y, in0=prod[:, 0:512], in1=prod[:, 512:1024], op=ALU.add)
            else:
                nc.gpsimd.tensor_tensor(out=y, in0=prod[:, 0:512], in1=prod[:, 512:1024], op=ALU.add)
            nc.sync.dma_start(out=outs[g // 2][P * m : P * m + P, 512 * half : 512 * half + 512], in_=y)

        vaccs = {}

        def value_mm(i):
            vaccs[i] = project(accvp, i // 2, 4 + i % 2)

        def value_out(i):
            m = i // 2
            half = i % 2
            if half == 0:
                pair["v"] = vp.tile([P, 1024], F32, name="v")
            nc.scalar.copy(out=pair["v"][:, 512 * half : 512 * half + 512], in_=vaccs[i])
            if half == 1:
                nc.sync.dma_start(out=outs[2][P * m : P * m + P, :], in_=pair["v"])

        banks = [(m, g) for g in range(4) for m in range(8)]
        accs = {}

        table_angles(0)
        table_sines(0)
        table_angles(1)
        tx(0)
        cpx(0, "v")
        tw(0, 0)
        tw(0, 1)
        cpw(0, 0, "s")
        cpw(0, 1, "v")
        quant_x(0, 1)
        finish_table(0)
        quant_w0(0)
        acc0 = [accp.tile([P, 256], F32, name="acc") for f in range(2)]
        accs[0] = acc0
        tw(0, 2)
        tw(0, 3)
        project0(acc0[0], 0)
        cpw(0, 2, "s")
        cpw(0, 3, "v")
        quant_w0(1)
        tx(1)
        project0(acc0[1], 1)
        cpx(1, "s")
        tx(2)
        tx(3)
        cpx(2, "s")
        cpx(3, "s")
        quant_x(1, 2)
        tx(4)
        tx(5)
        accs[1] = project(accp, 1, 0)
        cpx(4, "s")
        cpx(5, "s")
        quant_x(2, 4)
        tx(6)
        tx(7)
        cpx(6, "s")
        cpx(7, "s")

        for k in range(32):
            if k == 1:
                quant_x(4, 8)
            if k == FIN1 and not FIN1_ACT:
                finish_table(1)
            if k in WQ:
                quant_w(WQ[k], 1)
            if k + LOOK < 32:
                accs[k + LOOK] = project(accp, banks[k + LOOK][0], banks[k + LOOK][1])
            if k >= V0 and k - V0 < 16:
                value_mm(k - V0)
            if k == 2:
                table_sines(1)
                if FIN1_ACT:
                    finish_table_act(1)
            for d, js in ((LEAD, (0, 1)), (LEAD - 1, (2, 3))):
                if k + d in WQ:
                    for j in js:
                        tw(WQ[k + d], j)
                    for j in js:
                        cpw(WQ[k + d], j, "s")
            if k >= V0 and k - V0 < 16:
                value_out(k - V0)
            rotate(k, banks[k][0], banks[k][1], accs[k])
